import numpy as np
import ml_dtypes


def mxq(x, axis, fmt="e4m3"):
    dtype, down = {"e4m3": (ml_dtypes.float8_e4m3fn, 7), "e5m2": (ml_dtypes.float8_e5m2, 14)}[fmt]
    v = np.moveaxis(np.asarray(x, np.float32).astype(ml_dtypes.bfloat16).astype(np.float64), axis, -1)
    blocks = v.reshape(v.shape[:-1] + (-1, 32))
    amax = np.abs(blocks).max(-1, keepdims=True)
    byte = np.maximum(np.where(amax > 0, np.frexp(amax)[1] - 1 + 127, 0) - down, 1)
    scale = np.exp2(byte - 127.0)
    codes = (blocks / scale).astype(np.float32).astype(dtype).astype(np.float64)
    return np.moveaxis((codes * scale).reshape(v.shape), -1, axis)


WIDE = False


def mx_kscale(k):
    if not WIDE:
        return np.ones(k)
    levels = np.array([20, -20, 10, -10, 0])
    a = np.random.permutation(np.resize(levels, k // 512 * 4)).reshape(k // 512, 4)
    idx = np.arange(k)
    return np.exp2(a[idx // 512, idx % 128 // 32])


BF16 = ml_dtypes.bfloat16


def bf(x):
    return np.asarray(x, np.float32).astype(BF16)


def f64(x):
    return np.asarray(x).astype(np.float64)


B, N, SIZE, CH = 128, 16, 1024, 512


def sigmoid(v):
    return 1.0 / (1.0 + np.exp(-v))


def setup_inputs():
    u = mx_kscale(CH)
    half = np.concatenate([np.ones(CH), np.full(CH, 2.0 / np.sqrt(N))])
    z_node = bf(np.random.standard_normal((B, N, SIZE)))
    z_children = bf(np.random.standard_normal((B, N, SIZE)) * half)
    W0 = bf(np.random.standard_normal((CH, SIZE)) / np.sqrt(SIZE))
    U_f = bf(np.random.standard_normal((CH, CH)) / np.sqrt(CH))
    b_f = bf(np.random.standard_normal(CH) * 0.5)
    g = bf(np.random.standard_normal((B, CH)) * np.exp2(np.random.randint(-12, 1, (B, 1))) * 256.0 * u)
    f_gate = sigmoid(f64(z_node) @ f64(W0).T + f64(z_children)[..., :CH] @ f64(U_f).T + f64(b_f))
    return {"z_node": z_node,
            "z_children": z_children,
            "W_f": bf(f64(W0) / u[:, None]),
            "U_f": U_f,
            "b_f": b_f,
            "f_gate": np.asarray(f_gate, np.float32),
            "grad_out": g}


def reference(z_node, z_children, W_f, U_f, b_f, f_gate, grad_out):
    c_k = f64(z_children)[..., CH:]
    f = f64(f_gate)
    da = f64(grad_out)[:, None, :] * (c_k * f * (1.0 - f))
    return mxq(da, 2, "e5m2") @ mxq(f64(W_f), 0, "e4m3")

@@ -1,0 +1,164 @@
+from contextlib import ExitStack
+
+import concourse.mybir as mybir
+from concourse.masks import make_identity
+
+F32 = mybir.dt.float32
+BF16 = mybir.dt.bfloat16
+U32 = mybir.dt.uint32
+U8 = mybir.dt.uint8
+E5M2_X4 = mybir.dt.float8_e5m2_x4
+E4M3_X4 = mybir.dt.float8_e4m3fn_x4
+ALU = mybir.AluOpType
+
+P = 128
+CHILDREN = 16
+CH = 512
+SIZE = 1024
+PACK = 4
+N_TILE = 512
+HALVES = SIZE // N_TILE
+PAIR = 2
+PAIRS = CHILDREN // PAIR
+W_STEP = 4
+
+FLOPS = 2 * P * CHILDREN * CH * SIZE
+BYTES = P * CHILDREN * CH * (4 + 2) + CH * SIZE * 2 + P * CH * 2 + P * CHILDREN * SIZE * 4
+
+
+def tile_treelstm_pa_v_kernel(tc, z_node, z_children, W_f, U_f, b_f, f_gate, grad_out, out):
+    nc = tc.nc
+    with ExitStack() as ctx:
+        keep = ctx.enter_context(tc.tile_pool(name="keep", bufs=1))
+        work = ctx.enter_context(tc.tile_pool(name="work", bufs=3))
+        psum_t = ctx.enter_context(tc.psum_pool(name="psum_t", bufs=3))
+        psum_o = ctx.enter_context(tc.psum_pool(name="psum_o", bufs=5))
+
+        f_sb = [keep.tile([P, PAIR, CH], F32, name="f_sb%d" % j) for j in range(PAIRS)]
+        ck_sb = [keep.tile([P, PAIR, CH], BF16, name="ck_sb%d" % j) for j in range(PAIRS)]
+        g_sb = keep.tile([P, CH], BF16)
+        w_raw = keep.tile([P, PACK, SIZE], BF16)
+
+        def load_gates(j):
+            nc.sync.dma_start(out=f_sb[j][:], in_=f_gate[:, j * PAIR : (j + 1) * PAIR, :])
+
+        def load_cells(j):
+            nc.sync.dma_start(out=ck_sb[j][:], in_=z_children[:, j * PAIR : (j + 1) * PAIR, CH:])
+
+        load_gates(0)
+        nc.sync.dma_start(out=g_sb[:], in_=grad_out)
+        load_cells(0)
+        load_gates(1)
+        load_cells(1)
+        nc.sync.dma_start(out=w_raw[:], in_=W_f.rearrange("(t p) s -> p t s", p=P))
+        for j in range(2, PAIRS):
+            load_gates(j)
+            load_cells(j)
+
+        ident = keep.tile([P, P], F32)
+        make_identity(nc, ident[:])
+
+        g_f32 = keep.tile([P, CH], F32)
+        nc.scalar.mul(out=g_f32[:], in_=g_sb[:], mul=-1.0)
+        g_ps = psum_t.tile([P, PACK, P], F32, tag="x_t")
+        for t in range(PACK):
+            nc.tensor.transpose(g_ps[:, t, :], g_f32[:, t * P : (t + 1) * P], ident[:])
+        g_t = keep.tile([P, P, PACK], F32)
+        nc.scalar.copy(out=g_t[:], in_=g_ps[:].rearrange("p t b -> p b t"))
+
+        w_grouped = keep.tile([P, SIZE, PACK], BF16, align_bytes=64)
+        w_codes = keep.tile([P, SIZE], U32, align_bytes=64)
+        w_scales = keep.tile([P, SIZE], U8, align_bytes=64)
+
+        def group_w(h):
+            cols = slice(h * N_TILE, (h + 1) * N_TILE)
+            nc.scalar.copy(out=w_grouped[:, cols, :], in_=w_raw[:, :, cols].rearrange("p t s -> p s t"))
+
+        def quantise_w(h):
+            cols = slice(h * N_TILE, (h + 1) * N_TILE)
+            nc.vector.quantize_mx(
+                out=w_codes[:, cols].bitcast(E4M3_X4),
+                scales=w_scales[:, cols],
+                in_=w_grouped[:, cols, :].rearrange("p s t -> p (s t)"),
+            )
+
+        da_codes = keep.tile([P, CHILDREN, P], U32, align_bytes=64)
+        da_scales = keep.tile([P, CHILDREN, P], U8, align_bytes=64)
+        slope = {}
+        x_sb = {}
+        x_t = {}
+        da_bf = {}
+
+        def gate_slope(j):
+            slope[j] = work.tile([P, PAIR, CH], F32, name="slope", tag="slope")
+            nc.vector.scalar_tensor_tensor(
+                out=slope[j][:], in0=f_sb[j][:], scalar=1.0, in1=f_sb[j][:],
+                op0=ALU.subtract, op1=ALU.mult,
+            )
+
+        def times_cell(j):
+            x_sb[j] = work.tile([P, PAIR, CH], F32, name="x_sb", tag="x_sb")
+            nc.vector.tensor_tensor(out=x_sb[j][:], in0=slope[j][:], in1=ck_sb[j][:], op=ALU.mult)
+
+        def transpose_pair(j):
+            for i in range(PAIR):
+                n = j * PAIR + i
+                x_t[n] = psum_t.tile([P, PACK, P], F32, name="x_t", tag="x_t")
+                for t in range(PACK):
+                    nc.tensor.transpose(x_t[n][:, t, :], x_sb[j][:, i, t * P : (t + 1) * P], ident[:])
+
+        def times_grad(n):
+            da_bf[n] = work.tile([P, P, PACK], BF16, name="da_bf", tag="da_bf", align_bytes=64)
+            nc.vector.tensor_tensor(
+                out=da_bf[n][:], in0=x_t[n][:].rearrange("p t b -> p b t"), in1=g_t[:], op=ALU.mult
+            )
+
+        def quantise(n):
+            nc.vector.quantize_mx(
+                out=da_codes[:, n, :].bitcast(E5M2_X4),
+                scales=da_scales[:, n, :],
+                in_=da_bf[n][:].rearrange("p b t -> p (b t)"),
+            )
+
+        def multiply(n):
+            out_sb = keep.tile([P, SIZE], F32, name="out_sb%d" % n)
+            for h in range(HALVES):
+                cols = slice(h * N_TILE, (h + 1) * N_TILE)
+                acc = psum_o.tile([P, N_TILE], F32, name="acc", tag="acc")
+                nc.tensor.matmul_mx(
+                    out=acc[:],
+                    lhsT=da_codes[:, n, :].bitcast(E5M2_X4),
+                    lhsT_scale=da_scales[:, n, :],
+                    rhs=w_codes[:, cols].bitcast(E4M3_X4),
+                    rhs_scale=w_scales[:, cols],
+                    start=True,
+                    stop=True,
+                )
+                nc.scalar.copy(out=out_sb[:, cols], in_=acc[:])
+            nc.sync.dma_start(out=out[:, n, :], in_=out_sb[:])
+
+        gate_slope(0)
+        times_cell(0)
+        transpose_pair(0)
+        for h in range(HALVES):
+            group_w(h)
+        multiplied = 0
+        for n in range(CHILDREN):
+            ahead = n // PAIR + 1
+            if ahead < PAIRS and n % PAIR == 0:
+                gate_slope(ahead)
+            if ahead < PAIRS and n % PAIR == 1:
+                times_cell(ahead)
+                transpose_pair(ahead)
+            times_grad(n)
+            if n > 0:
+                quantise(n - 1)
+            if n == W_STEP:
+                for h in range(HALVES):
+                    quantise_w(h)
+            if n >= W_STEP:
+                for m in range(multiplied, n):
+                    multiply(m)
+                multiplied = n
+        quantise(CHILDREN - 1)
+        multiply(CHILDREN - 1)

@@ -33,6 +33,7 @@ def tile_treelstm_pa_v_kernel(tc, z_node, z_children, W_f, U_f, b_f, f_gate, gra
         work = ctx.enter_context(tc.tile_pool(name="work", bufs=3))
         psum_t = ctx.enter_context(tc.psum_pool(name="psum_t", bufs=3))
         psum_o = ctx.enter_context(tc.psum_pool(name="psum_o", bufs=5))
+        ctx.enter_context(tc.manual_schedule())
 
         f_sb = [keep.tile([P, PAIR, CH], F32, name="f_sb%d" % j) for j in range(PAIRS)]
         ck_sb = [keep.tile([P, PAIR, CH], BF16, name="ck_sb%d" % j) for j in range(PAIRS)]

@@ -21,6 +21,7 @@ HALVES = SIZE // N_TILE
 PAIR = 2
 PAIRS = CHILDREN // PAIR
 W_STEP = 4
+TAIL = PAIR
 
 FLOPS = 2 * P * CHILDREN * CH * SIZE
 BYTES = P * CHILDREN * CH * (4 + 2) + CH * SIZE * 2 + P * CH * 2 + P * CHILDREN * SIZE * 4
@@ -121,7 +122,7 @@ def tile_treelstm_pa_v_kernel(tc, z_node, z_children, W_f, U_f, b_f, f_gate, gra
                 in_=da_bf[n][:].rearrange("p b t -> p (b t)"),
             )
 
-        def multiply(n):
+        def multiply(n, vector_helps):
             out_sb = keep.tile([P, SIZE], F32, name="out_sb%d" % n)
             for h in range(HALVES):
                 cols = slice(h * N_TILE, (h + 1) * N_TILE)
@@ -135,7 +136,10 @@ def tile_treelstm_pa_v_kernel(tc, z_node, z_children, W_f, U_f, b_f, f_gate, gra
                     start=True,
                     stop=True,
                 )
-                nc.scalar.copy(out=out_sb[:, cols], in_=acc[:])
+                if vector_helps and h == HALVES - 1:
+                    nc.vector.tensor_copy(out=out_sb[:, cols], in_=acc[:])
+                else:
+                    nc.scalar.copy(out=out_sb[:, cols], in_=acc[:])
             nc.sync.dma_start(out=out[:, n, :], in_=out_sb[:])
 
         gate_slope(0)
@@ -158,8 +162,10 @@ def tile_treelstm_pa_v_kernel(tc, z_node, z_children, W_f, U_f, b_f, f_gate, gra
                 for h in range(HALVES):
                     quantise_w(h)
             if n >= W_STEP:
-                for m in range(multiplied, n):
-                    multiply(m)
-                multiplied = n
+                due = min(n, CHILDREN - TAIL)
+                for m in range(multiplied, due):
+                    multiply(m, vector_helps=False)
+                multiplied = due
         quantise(CHILDREN - 1)
-        multiply(CHILDREN - 1)
+        for m in range(CHILDREN - TAIL, CHILDREN):
+            multiply(m, vector_helps=True)

@@ -20,8 +20,9 @@ N_TILE = 512
 HALVES = SIZE // N_TILE
 PAIR = 2
 PAIRS = CHILDREN // PAIR
-W_STEP = 4
-TAIL = PAIR
+W_PAIR = 2
+CATCH_UP = 3
+GPSIMD_COLS = 384
 
 FLOPS = 2 * P * CHILDREN * CH * SIZE
 BYTES = P * CHILDREN * CH * (4 + 2) + CH * SIZE * 2 + P * CH * 2 + P * CHILDREN * SIZE * 4
@@ -52,8 +53,10 @@ def tile_treelstm_pa_v_kernel(tc, z_node, z_children, W_f, U_f, b_f, f_gate, gra
         load_cells(0)
         load_gates(1)
         load_cells(1)
+        load_gates(2)
         nc.sync.dma_start(out=w_raw[:], in_=W_f.rearrange("(t p) s -> p t s", p=P))
-        for j in range(2, PAIRS):
+        load_cells(2)
+        for j in range(3, PAIRS):
             load_gates(j)
             load_cells(j)
 
@@ -93,14 +96,19 @@ def tile_treelstm_pa_v_kernel(tc, z_node, z_children, W_f, U_f, b_f, f_gate, gra
 
         def gate_slope(j):
             slope[j] = work.tile([P, PAIR, CH], F32, name="slope", tag="slope")
+            x_sb[j] = work.tile([P, PAIR, CH], F32, name="x_sb", tag="x_sb")
             nc.vector.scalar_tensor_tensor(
                 out=slope[j][:], in0=f_sb[j][:], scalar=1.0, in1=f_sb[j][:],
                 op0=ALU.subtract, op1=ALU.mult,
             )
 
-        def times_cell(j):
-            x_sb[j] = work.tile([P, PAIR, CH], F32, name="x_sb", tag="x_sb")
-            nc.vector.tensor_tensor(out=x_sb[j][:], in0=slope[j][:], in1=ck_sb[j][:], op=ALU.mult)
+        def times_cell(engine, j, cols):
+            engine.tensor_tensor(
+                out=x_sb[j][:].rearrange("p k c -> p (k c)")[:, cols],
+                in0=slope[j][:].rearrange("p k c -> p (k c)")[:, cols],
+                in1=ck_sb[j][:].rearrange("p k c -> p (k c)")[:, cols],
+                op=ALU.mult,
+            )
 
         def transpose_pair(j):
             for i in range(PAIR):
@@ -143,29 +151,30 @@ def tile_treelstm_pa_v_kernel(tc, z_node, z_children, W_f, U_f, b_f, f_gate, gra
             nc.sync.dma_start(out=out[:, n, :], in_=out_sb[:])
 
         gate_slope(0)
-        times_cell(0)
+        times_cell(nc.vector, 0, slice(0, PAIR * CH))
         transpose_pair(0)
         for h in range(HALVES):
             group_w(h)
         multiplied = 0
-        for n in range(CHILDREN):
-            ahead = n // PAIR + 1
-            if ahead < PAIRS and n % PAIR == 0:
-                gate_slope(ahead)
-            if ahead < PAIRS and n % PAIR == 1:
-                times_cell(ahead)
-                transpose_pair(ahead)
-            times_grad(n)
-            if n > 0:
-                quantise(n - 1)
-            if n == W_STEP:
+        for j in range(PAIRS):
+            kids = range(j * PAIR, (j + 1) * PAIR)
+            more = j + 1 < PAIRS
+            if more:
+                gate_slope(j + 1)
+                times_cell(nc.gpsimd, j + 1, slice(PAIR * CH - GPSIMD_COLS, PAIR * CH))
+            for n in kids:
+                times_grad(n)
+            if more:
+                times_cell(nc.vector, j + 1, slice(0, PAIR * CH - GPSIMD_COLS))
+                transpose_pair(j + 1)
+            for n in kids:
+                quantise(n)
+            if j == W_PAIR:
                 for h in range(HALVES):
                     quantise_w(h)
-            if n >= W_STEP:
-                due = min(n, CHILDREN - TAIL)
+            if j >= W_PAIR:
+                due = min((j + 1) * PAIR, multiplied + CATCH_UP)
                 for m in range(multiplied, due):
-                    multiply(m, vector_helps=False)
+                    multiply(m, vector_helps=not more)
                 multiplied = due
-        quantise(CHILDREN - 1)
-        for m in range(CHILDREN - TAIL, CHILDREN):
-            multiply(m, vector_helps=True)
+        assert multiplied == CHILDREN

@@ -20,8 +20,10 @@ N_TILE = 512
 HALVES = SIZE // N_TILE
 PAIR = 2
 PAIRS = CHILDREN // PAIR
-W_PAIR = 2
+W_PAIR = 1
 CATCH_UP = 3
+FINE_FROM = 12
+VECTOR_FROM = 13
 GPSIMD_COLS = 384
 
 FLOPS = 2 * P * CHILDREN * CH * SIZE
@@ -48,13 +50,16 @@ def tile_treelstm_pa_v_kernel(tc, z_node, z_children, W_f, U_f, b_f, f_gate, gra
         def load_cells(j):
             nc.sync.dma_start(out=ck_sb[j][:], in_=z_children[:, j * PAIR : (j + 1) * PAIR, CH:])
 
-        load_gates(0)
-        nc.sync.dma_start(out=g_sb[:], in_=grad_out)
+        for i in range(PAIR):
+            nc.sync.dma_start(out=f_sb[0][:, i, :], in_=f_gate[:, i, :])
         load_cells(0)
+        nc.sync.dma_start(out=g_sb[:], in_=grad_out)
+        w_view = W_f.rearrange("(t p) s -> p t s", p=P)
         load_gates(1)
         load_cells(1)
+        nc.sync.dma_start(out=w_raw[:, :, :N_TILE], in_=w_view[:, :, :N_TILE])
         load_gates(2)
-        nc.sync.dma_start(out=w_raw[:], in_=W_f.rearrange("(t p) s -> p t s", p=P))
+        nc.sync.dma_start(out=w_raw[:, :, N_TILE:], in_=w_view[:, :, N_TILE:])
         load_cells(2)
         for j in range(3, PAIRS):
             load_gates(j)
@@ -94,13 +99,15 @@ def tile_treelstm_pa_v_kernel(tc, z_node, z_children, W_f, U_f, b_f, f_gate, gra
         x_t = {}
         da_bf = {}
 
-        def gate_slope(j):
+        def gate_slope(j, pieces=1):
             slope[j] = work.tile([P, PAIR, CH], F32, name="slope", tag="slope")
             x_sb[j] = work.tile([P, PAIR, CH], F32, name="x_sb", tag="x_sb")
-            nc.vector.scalar_tensor_tensor(
-                out=slope[j][:], in0=f_sb[j][:], scalar=1.0, in1=f_sb[j][:],
-                op0=ALU.subtract, op1=ALU.mult,
-            )
+            step = PAIR // pieces
+            for i in range(0, PAIR, step):
+                nc.vector.scalar_tensor_tensor(
+                    out=slope[j][:, i : i + step, :], in0=f_sb[j][:, i : i + step, :], scalar=1.0,
+                    in1=f_sb[j][:, i : i + step, :], op0=ALU.subtract, op1=ALU.mult,
+                )
 
         def times_cell(engine, j, cols):
             engine.tensor_tensor(
@@ -118,19 +125,24 @@ def tile_treelstm_pa_v_kernel(tc, z_node, z_children, W_f, U_f, b_f, f_gate, gra
                     nc.tensor.transpose(x_t[n][:, t, :], x_sb[j][:, i, t * P : (t + 1) * P], ident[:])
 
         def times_grad(n):
-            da_bf[n] = work.tile([P, P, PACK], BF16, name="da_bf", tag="da_bf", align_bytes=64)
+            j, i = divmod(n, PAIR)
+            if i == 0:
+                da_bf[j] = work.tile([P, PAIR, P, PACK], BF16, name="da_bf", tag="da_bf", align_bytes=64)
             nc.vector.tensor_tensor(
-                out=da_bf[n][:], in0=x_t[n][:].rearrange("p t b -> p b t"), in1=g_t[:], op=ALU.mult
+                out=da_bf[j][:, i], in0=x_t[n][:].rearrange("p t b -> p b t"), in1=g_t[:], op=ALU.mult
             )
 
-        def quantise(n):
+        def quantise_pair(j):
+            kids = slice(j * PAIR, (j + 1) * PAIR)
             nc.vector.quantize_mx(
-                out=da_codes[:, n, :].bitcast(E5M2_X4),
-                scales=da_scales[:, n, :],
-                in_=da_bf[n][:].rearrange("p b t -> p (b t)"),
+                out=da_codes[:, kids, :].rearrange("p k b -> p (k b)").bitcast(E5M2_X4),
+                scales=da_scales[:, kids, :].rearrange("p k b -> p (k b)"),
+                in_=da_bf[j][:].rearrange("p k b t -> p (k b t)"),
             )
 
-        def multiply(n, vector_helps):
+        waiting = []
+
+        def multiply(n):
             out_sb = keep.tile([P, SIZE], F32, name="out_sb%d" % n)
             for h in range(HALVES):
                 cols = slice(h * N_TILE, (h + 1) * N_TILE)
@@ -144,13 +156,23 @@ def tile_treelstm_pa_v_kernel(tc, z_node, z_children, W_f, U_f, b_f, f_gate, gra
                     start=True,
                     stop=True,
                 )
-                if vector_helps and h == HALVES - 1:
-                    nc.vector.tensor_copy(out=out_sb[:, cols], in_=acc[:])
+                if n >= VECTOR_FROM and h == HALVES - 1:
+                    waiting.append((n, out_sb, acc))
                 else:
                     nc.scalar.copy(out=out_sb[:, cols], in_=acc[:])
-            nc.sync.dma_start(out=out[:, n, :], in_=out_sb[:])
+                    if n >= FINE_FROM:
+                        nc.sync.dma_start(out=out[:, n, cols], in_=out_sb[:, cols])
+            if n < FINE_FROM:
+                nc.sync.dma_start(out=out[:, n, :], in_=out_sb[:])
 
-        gate_slope(0)
+        def vector_empties():
+            cols = slice(N_TILE, SIZE)
+            for n, out_sb, acc in waiting:
+                nc.vector.tensor_copy(out=out_sb[:, cols], in_=acc[:])
+                nc.sync.dma_start(out=out[:, n, cols], in_=out_sb[:, cols])
+            waiting.clear()
+
+        gate_slope(0, pieces=PAIR)
         times_cell(nc.vector, 0, slice(0, PAIR * CH))
         transpose_pair(0)
         for h in range(HALVES):
@@ -167,14 +189,15 @@ def tile_treelstm_pa_v_kernel(tc, z_node, z_children, W_f, U_f, b_f, f_gate, gra
             if more:
                 times_cell(nc.vector, j + 1, slice(0, PAIR * CH - GPSIMD_COLS))
                 transpose_pair(j + 1)
-            for n in kids:
-                quantise(n)
+            quantise_pair(j)
             if j == W_PAIR:
                 for h in range(HALVES):
                     quantise_w(h)
             if j >= W_PAIR:
                 due = min((j + 1) * PAIR, multiplied + CATCH_UP)
                 for m in range(multiplied, due):
-                    multiply(m, vector_helps=not more)
+                    multiply(m)
                 multiplied = due
+                if not more:
+                    vector_empties()
         assert multiplied == CHILDREN

@@ -22,6 +22,7 @@ PAIR = 2
 PAIRS = CHILDREN // PAIR
 W_PAIR = 1
 CATCH_UP = 3
+COARSE_BELOW = 10
 FINE_FROM = 12
 VECTOR_FROM = 13
 GPSIMD_COLS = 384
@@ -39,19 +40,23 @@ def tile_treelstm_pa_v_kernel(tc, z_node, z_children, W_f, U_f, b_f, f_gate, gra
         psum_o = ctx.enter_context(tc.psum_pool(name="psum_o", bufs=5))
         ctx.enter_context(tc.manual_schedule())
 
-        f_sb = [keep.tile([P, PAIR, CH], F32, name="f_sb%d" % j) for j in range(PAIRS)]
-        ck_sb = [keep.tile([P, PAIR, CH], BF16, name="ck_sb%d" % j) for j in range(PAIRS)]
+        f_all = keep.tile([P, CHILDREN, CH], F32)
+        ck_all = keep.tile([P, CHILDREN, CH], BF16)
+        f_sb = [f_all[:, j * PAIR : (j + 1) * PAIR, :] for j in range(PAIRS)]
+        ck_sb = [ck_all[:, j * PAIR : (j + 1) * PAIR, :] for j in range(PAIRS)]
         g_sb = keep.tile([P, CH], BF16)
         w_raw = keep.tile([P, PACK, SIZE], BF16)
 
-        def load_gates(j):
-            nc.sync.dma_start(out=f_sb[j][:], in_=f_gate[:, j * PAIR : (j + 1) * PAIR, :])
+        def load_gates(j, pairs=1):
+            kids = slice(j * PAIR, (j + pairs) * PAIR)
+            nc.sync.dma_start(out=f_all[:, kids, :], in_=f_gate[:, kids, :])
 
-        def load_cells(j):
-            nc.sync.dma_start(out=ck_sb[j][:], in_=z_children[:, j * PAIR : (j + 1) * PAIR, CH:])
+        def load_cells(j, pairs=1):
+            kids = slice(j * PAIR, (j + pairs) * PAIR)
+            nc.sync.dma_start(out=ck_all[:, kids, :], in_=z_children[:, kids, CH:])
 
         for i in range(PAIR):
-            nc.sync.dma_start(out=f_sb[0][:, i, :], in_=f_gate[:, i, :])
+            nc.sync.dma_start(out=f_all[:, i, :], in_=f_gate[:, i, :])
         load_cells(0)
         nc.sync.dma_start(out=g_sb[:], in_=grad_out)
         w_view = W_f.rearrange("(t p) s -> p t s", p=P)
@@ -61,9 +66,11 @@ def tile_treelstm_pa_v_kernel(tc, z_node, z_children, W_f, U_f, b_f, f_gate, gra
         load_gates(2)
         nc.sync.dma_start(out=w_raw[:, :, N_TILE:], in_=w_view[:, :, N_TILE:])
         load_cells(2)
-        for j in range(3, PAIRS):
-            load_gates(j)
-            load_cells(j)
+        load_gates(3)
+        load_cells(3)
+        for j in range(4, PAIRS, 2):
+            load_gates(j, pairs=2)
+            load_cells(j, pairs=2)
 
         ident = keep.tile([P, P], F32)
         make_identity(nc, ident[:])
@@ -113,7 +120,7 @@ def tile_treelstm_pa_v_kernel(tc, z_node, z_children, W_f, U_f, b_f, f_gate, gra
             engine.tensor_tensor(
                 out=x_sb[j][:].rearrange("p k c -> p (k c)")[:, cols],
                 in0=slope[j][:].rearrange("p k c -> p (k c)")[:, cols],
-                in1=ck_sb[j][:].rearrange("p k c -> p (k c)")[:, cols],
+                in1=ck_sb[j].rearrange("p k c -> p (k c)")[:, cols],
                 op=ALU.mult,
             )
 
@@ -142,8 +149,13 @@ def tile_treelstm_pa_v_kernel(tc, z_node, z_children, W_f, U_f, b_f, f_gate, gra
 
         waiting = []
 
+        out_pair = {}
+
         def multiply(n):
-            out_sb = keep.tile([P, SIZE], F32, name="out_sb%d" % n)
+            j, i = divmod(n, PAIR)
+            if i == 0:
+                out_pair[j] = keep.tile([P, PAIR, SIZE], F32, name="out_pair%d" % j)
+            out_sb = out_pair[j][:, i, :]
             for h in range(HALVES):
                 cols = slice(h * N_TILE, (h + 1) * N_TILE)
                 acc = psum_o.tile([P, N_TILE], F32, name="acc", tag="acc")
@@ -162,8 +174,11 @@ def tile_treelstm_pa_v_kernel(tc, z_node, z_children, W_f, U_f, b_f, f_gate, gra
                     nc.scalar.copy(out=out_sb[:, cols], in_=acc[:])
                     if n >= FINE_FROM:
                         nc.sync.dma_start(out=out[:, n, cols], in_=out_sb[:, cols])
-            if n < FINE_FROM:
-                nc.sync.dma_start(out=out[:, n, :], in_=out_sb[:])
+            if n < COARSE_BELOW:
+                if i == PAIR - 1:
+                    nc.sync.dma_start(out=out[:, j * PAIR : (j + 1) * PAIR, :], in_=out_pair[j][:])
+            elif n < FINE_FROM:
+                nc.sync.dma_start(out=out[:, n, :], in_=out_sb)
 
         def vector_empties():
             cols = slice(N_TILE, SIZE)

@@ -124,12 +124,15 @@ def tile_treelstm_pa_v_kernel(tc, z_node, z_children, W_f, U_f, b_f, f_gate, gra
                 op=ALU.mult,
             )
 
+        def transpose_child(n):
+            j, i = divmod(n, PAIR)
+            x_t[n] = psum_t.tile([P, PACK, P], F32, name="x_t", tag="x_t")
+            for t in range(PACK):
+                nc.tensor.transpose(x_t[n][:, t, :], x_sb[j][:, i, t * P : (t + 1) * P], ident[:])
+
         def transpose_pair(j):
             for i in range(PAIR):
-                n = j * PAIR + i
-                x_t[n] = psum_t.tile([P, PACK, P], F32, name="x_t", tag="x_t")
-                for t in range(PACK):
-                    nc.tensor.transpose(x_t[n][:, t, :], x_sb[j][:, i, t * P : (t + 1) * P], ident[:])
+                transpose_child(j * PAIR + i)
 
         def times_grad(n):
             j, i = divmod(n, PAIR)
@@ -197,13 +200,15 @@ def tile_treelstm_pa_v_kernel(tc, z_node, z_children, W_f, U_f, b_f, f_gate, gra
             kids = range(j * PAIR, (j + 1) * PAIR)
             more = j + 1 < PAIRS
             if more:
-                gate_slope(j + 1)
+                gate_slope(j + 1, pieces=PAIR)
                 times_cell(nc.gpsimd, j + 1, slice(PAIR * CH - GPSIMD_COLS, PAIR * CH))
+                times_cell(nc.vector, j + 1, slice(0, CH))
+                transpose_child((j + 1) * PAIR)
             for n in kids:
                 times_grad(n)
             if more:
-                times_cell(nc.vector, j + 1, slice(0, PAIR * CH - GPSIMD_COLS))
-                transpose_pair(j + 1)
+                times_cell(nc.vector, j + 1, slice(CH, PAIR * CH - GPSIMD_COLS))
+                transpose_child((j + 1) * PAIR + 1)
             quantise_pair(j)
             if j == W_PAIR:
                 for h in range(HALVES):

@@ -25,7 +25,7 @@ CATCH_UP = 3
 COARSE_BELOW = 10
 FINE_FROM = 12
 VECTOR_FROM = 13
-GPSIMD_COLS = 384
+GPSIMD_COLS = 512
 
 FLOPS = 2 * P * CHILDREN * CH * SIZE
 BYTES = P * CHILDREN * CH * (4 + 2) + CH * SIZE * 2 + P * CH * 2 + P * CHILDREN * SIZE * 4
@@ -207,7 +207,8 @@ def tile_treelstm_pa_v_kernel(tc, z_node, z_children, W_f, U_f, b_f, f_gate, gra
             for n in kids:
                 times_grad(n)
             if more:
-                times_cell(nc.vector, j + 1, slice(CH, PAIR * CH - GPSIMD_COLS))
+                if GPSIMD_COLS < CH:
+                    times_cell(nc.vector, j + 1, slice(CH, PAIR * CH - GPSIMD_COLS))
                 transpose_child((j + 1) * PAIR + 1)
             quantise_pair(j)
             if j == W_PAIR:

@@ -116,6 +116,15 @@ def tile_treelstm_pa_v_kernel(tc, z_node, z_children, W_f, U_f, b_f, f_gate, gra
                     in1=f_sb[j][:, i : i + step, :], op0=ALU.subtract, op1=ALU.mult,
                 )
 
+        def gate_slope_child(j, i):
+            if i == 0:
+                slope[j] = work.tile([P, PAIR, CH], F32, name="slope", tag="slope")
+                x_sb[j] = work.tile([P, PAIR, CH], F32, name="x_sb", tag="x_sb")
+            nc.vector.scalar_tensor_tensor(
+                out=slope[j][:, i, :], in0=f_sb[j][:, i, :], scalar=1.0, in1=f_sb[j][:, i, :],
+                op0=ALU.subtract, op1=ALU.mult,
+            )
+
         def times_cell(engine, j, cols):
             engine.tensor_tensor(
                 out=x_sb[j][:].rearrange("p k c -> p (k c)")[:, cols],
@@ -195,30 +204,36 @@ def tile_treelstm_pa_v_kernel(tc, z_node, z_children, W_f, U_f, b_f, f_gate, gra
         transpose_pair(0)
         for h in range(HALVES):
             group_w(h)
-        multiplied = 0
-        for j in range(PAIRS):
-            kids = range(j * PAIR, (j + 1) * PAIR)
-            more = j + 1 < PAIRS
-            if more:
-                gate_slope(j + 1, pieces=PAIR)
-                times_cell(nc.gpsimd, j + 1, slice(PAIR * CH - GPSIMD_COLS, PAIR * CH))
-                times_cell(nc.vector, j + 1, slice(0, CH))
-                transpose_child((j + 1) * PAIR)
-            for n in kids:
-                times_grad(n)
-            if more:
-                if GPSIMD_COLS < CH:
-                    times_cell(nc.vector, j + 1, slice(CH, PAIR * CH - GPSIMD_COLS))
-                transpose_child((j + 1) * PAIR + 1)
+        state = {"multiplied": 0}
+
+        def finish_pair(j):
             quantise_pair(j)
             if j == W_PAIR:
                 for h in range(HALVES):
                     quantise_w(h)
             if j >= W_PAIR:
-                due = min((j + 1) * PAIR, multiplied + CATCH_UP)
-                for m in range(multiplied, due):
+                due = min((j + 1) * PAIR, state["multiplied"] + CATCH_UP)
+                for m in range(state["multiplied"], due):
                     multiply(m)
-                multiplied = due
-                if not more:
-                    vector_empties()
+                state["multiplied"] = due
+
+        for j in range(PAIRS):
+            kids = range(j * PAIR, (j + 1) * PAIR)
+            more = j + 1 < PAIRS
+            if more:
+                gate_slope_child(j + 1, 0)
+            if j > 0:
+                finish_pair(j - 1)
+            if more:
+                gate_slope_child(j + 1, 1)
+                times_cell(nc.gpsimd, j + 1, slice(CH, PAIR * CH))
+                times_cell(nc.vector, j + 1, slice(0, CH))
+                transpose_child((j + 1) * PAIR)
+            for n in kids:
+                times_grad(n)
+            if more:
+                transpose_child((j + 1) * PAIR + 1)
+        finish_pair(PAIRS - 1)
+        vector_empties()
+        multiplied = state["multiplied"]
         assert multiplied == CHILDREN

@@ -60,12 +60,13 @@ def tile_treelstm_pa_v_kernel(tc, z_node, z_children, W_f, U_f, b_f, f_gate, gra
         load_cells(0)
         nc.sync.dma_start(out=g_sb[:], in_=grad_out)
         w_view = W_f.rearrange("(t p) s -> p t s", p=P)
-        load_gates(1)
+        for i in range(PAIR, 2 * PAIR):
+            nc.sync.dma_start(out=f_all[:, i, :], in_=f_gate[:, i, :])
         load_cells(1)
         nc.sync.dma_start(out=w_raw[:, :, :N_TILE], in_=w_view[:, :, :N_TILE])
         load_gates(2)
-        nc.sync.dma_start(out=w_raw[:, :, N_TILE:], in_=w_view[:, :, N_TILE:])
         load_cells(2)
+        nc.sync.dma_start(out=w_raw[:, :, N_TILE:], in_=w_view[:, :, N_TILE:])
         load_gates(3)
         load_cells(3)
         for j in range(4, PAIRS, 2):
@@ -159,6 +160,14 @@ def tile_treelstm_pa_v_kernel(tc, z_node, z_children, W_f, U_f, b_f, f_gate, gra
                 in_=da_bf[j][:].rearrange("p k b t -> p (k b t)"),
             )
 
+        def quantise_child(n):
+            j, i = divmod(n, PAIR)
+            nc.vector.quantize_mx(
+                out=da_codes[:, n, :].bitcast(E5M2_X4),
+                scales=da_scales[:, n, :],
+                in_=da_bf[j][:, i].rearrange("p b t -> p (b t)"),
+            )
+
         waiting = []
 
         out_pair = {}
@@ -192,6 +201,35 @@ def tile_treelstm_pa_v_kernel(tc, z_node, z_children, W_f, U_f, b_f, f_gate, gra
             elif n < FINE_FROM:
                 nc.sync.dma_start(out=out[:, n, :], in_=out_sb)
 
+        def passes(n):
+            j, i = divmod(n, PAIR)
+            if i == 0:
+                out_pair[j] = keep.tile([P, PAIR, SIZE], F32, name="out_pair%d" % j)
+            banks = []
+            for h in range(HALVES):
+                cols = slice(h * N_TILE, (h + 1) * N_TILE)
+                acc = psum_o.tile([P, N_TILE], F32, name="acc", tag="acc")
+                nc.tensor.matmul_mx(
+                    out=acc[:],
+                    lhsT=da_codes[:, n, :].bitcast(E5M2_X4),
+                    lhsT_scale=da_scales[:, n, :],
+                    rhs=w_codes[:, cols].bitcast(E4M3_X4),
+                    rhs_scale=w_scales[:, cols],
+                    start=True,
+                    stop=True,
+                )
+                banks.append(acc)
+            return banks
+
+        def empty_and_store(on_vector, n, h, acc):
+            j, i = divmod(n, PAIR)
+            cols = slice(h * N_TILE, (h + 1) * N_TILE)
+            if on_vector:
+                nc.vector.tensor_copy(out=out_pair[j][:, i, cols], in_=acc[:])
+            else:
+                nc.scalar.copy(out=out_pair[j][:, i, cols], in_=acc[:])
+            nc.sync.dma_start(out=out[:, n, cols], in_=out_pair[j][:, i, cols])
+
         def vector_empties():
             cols = slice(N_TILE, SIZE)
             for n, out_sb, acc in waiting:
@@ -200,8 +238,9 @@ def tile_treelstm_pa_v_kernel(tc, z_node, z_children, W_f, U_f, b_f, f_gate, gra
             waiting.clear()
 
         gate_slope(0, pieces=PAIR)
-        times_cell(nc.vector, 0, slice(0, PAIR * CH))
-        transpose_pair(0)
+        for i in range(PAIR):
+            times_cell(nc.vector, 0, slice(i * CH, (i + 1) * CH))
+            transpose_child(i)
         for h in range(HALVES):
             group_w(h)
         state = {"multiplied": 0}
@@ -233,7 +272,27 @@ def tile_treelstm_pa_v_kernel(tc, z_node, z_children, W_f, U_f, b_f, f_gate, gra
                 times_grad(n)
             if more:
                 transpose_child((j + 1) * PAIR + 1)
-        finish_pair(PAIRS - 1)
-        vector_empties()
-        multiplied = state["multiplied"]
+            if j == PAIRS - 2:
+                break
+        last = CHILDREN - 2 * PAIR
+        assert state["multiplied"] == last
+        banks = {}
+        quantise_child(last)
+        banks[last] = passes(last)
+        empty_and_store(False, last, 0, banks[last][0])
+        empty_and_store(False, last, 1, banks[last][1])
+        times_grad(last + 2)
+        quantise_child(last + 1)
+        banks[last + 1] = passes(last + 1)
+        empty_and_store(False, last + 1, 0, banks[last + 1][0])
+        times_grad(last + 3)
+        quantise_child(last + 2)
+        banks[last + 2] = passes(last + 2)
+        quantise_child(last + 3)
+        banks[last + 3] = passes(last + 3)
+        empty_and_store(True, last + 1, 1, banks[last + 1][1])
+        for n in (last + 2, last + 3):
+            empty_and_store(False, n, 0, banks[n][0])
+            empty_and_store(True, n, 1, banks[n][1])
+        multiplied = CHILDREN
         assert multiplied == CHILDREN

@@ -136,9 +136,9 @@ def tile_treelstm_pa_v_kernel(tc, z_node, z_children, W_f, U_f, b_f, f_gate, gra
 
         def transpose_child(n):
             j, i = divmod(n, PAIR)
-            x_t[n] = psum_t.tile([P, PACK, P], F32, name="x_t", tag="x_t")
+            x_t[n] = psum_t.tile([P, P, PACK], F32, name="x_t", tag="x_t")
             for t in range(PACK):
-                nc.tensor.transpose(x_t[n][:, t, :], x_sb[j][:, i, t * P : (t + 1) * P], ident[:])
+                nc.tensor.transpose(x_t[n][:, :, t], x_sb[j][:, i, t * P : (t + 1) * P], ident[:])
 
         def transpose_pair(j):
             for i in range(PAIR):
@@ -149,7 +149,7 @@ def tile_treelstm_pa_v_kernel(tc, z_node, z_children, W_f, U_f, b_f, f_gate, gra
             if i == 0:
                 da_bf[j] = work.tile([P, PAIR, P, PACK], BF16, name="da_bf", tag="da_bf", align_bytes=64)
             nc.vector.tensor_tensor(
-                out=da_bf[j][:, i], in0=x_t[n][:].rearrange("p t b -> p b t"), in1=g_t[:], op=ALU.mult
+                out=da_bf[j][:, i], in0=x_t[n][:], in1=g_t[:], op=ALU.mult
             )
 
         def quantise_pair(j):

from contextlib import ExitStack

import concourse.mybir as mybir
from concourse.masks import make_identity

F32 = mybir.dt.float32
BF16 = mybir.dt.bfloat16
U32 = mybir.dt.uint32
U8 = mybir.dt.uint8
E5M2_X4 = mybir.dt.float8_e5m2_x4
E4M3_X4 = mybir.dt.float8_e4m3fn_x4
ALU = mybir.AluOpType

P = 128
CHILDREN = 16
CH = 512
SIZE = 1024
PACK = 4
N_TILE = 512
HALVES = SIZE // N_TILE
PAIR = 2
PAIRS = CHILDREN // PAIR
W_PAIR = 1
CATCH_UP = 3
COARSE_BELOW = 10
FINE_FROM = 12
VECTOR_FROM = 13
GPSIMD_COLS = 512

FLOPS = 2 * P * CHILDREN * CH * SIZE
BYTES = P * CHILDREN * CH * (4 + 2) + CH * SIZE * 2 + P * CH * 2 + P * CHILDREN * SIZE * 4


def tile_treelstm_pa_v_kernel(tc, z_node, z_children, W_f, U_f, b_f, f_gate, grad_out, out):
    nc = tc.nc
    with ExitStack() as ctx:
        keep = ctx.enter_context(tc.tile_pool(name="keep", bufs=1))
        work = ctx.enter_context(tc.tile_pool(name="work", bufs=3))
        psum_t = ctx.enter_context(tc.psum_pool(name="psum_t", bufs=3))
        psum_o = ctx.enter_context(tc.psum_pool(name="psum_o", bufs=5))
        ctx.enter_context(tc.manual_schedule())

        f_all = keep.tile([P, CHILDREN, CH], F32)
        ck_all = keep.tile([P, CHILDREN, CH], BF16)
        f_sb = [f_all[:, j * PAIR : (j + 1) * PAIR, :] for j in range(PAIRS)]
        ck_sb = [ck_all[:, j * PAIR : (j + 1) * PAIR, :] for j in range(PAIRS)]
        g_sb = keep.tile([P, CH], BF16)
        w_raw = keep.tile([P, PACK, SIZE], BF16)

        def load_gates(j, pairs=1):
            kids = slice(j * PAIR, (j + pairs) * PAIR)
            nc.sync.dma_start(out=f_all[:, kids, :], in_=f_gate[:, kids, :])

        def load_cells(j, pairs=1):
            kids = slice(j * PAIR, (j + pairs) * PAIR)
            nc.sync.dma_start(out=ck_all[:, kids, :], in_=z_children[:, kids, CH:])

        for i in range(PAIR):
            nc.sync.dma_start(out=f_all[:, i, :], in_=f_gate[:, i, :])
        load_cells(0)
        nc.sync.dma_start(out=g_sb[:], in_=grad_out)
        w_view = W_f.rearrange("(t p) s -> p t s", p=P)
        for i in range(PAIR, 2 * PAIR):
            nc.sync.dma_start(out=f_all[:, i, :], in_=f_gate[:, i, :])
        load_cells(1)
        nc.sync.dma_start(out=w_raw[:, :, :N_TILE], in_=w_view[:, :, :N_TILE])
        load_gates(2)
        load_cells(2)
        nc.sync.dma_start(out=w_raw[:, :, N_TILE:], in_=w_view[:, :, N_TILE:])
        load_gates(3)
        load_cells(3)
        for j in range(4, PAIRS, 2):
            load_gates(j, pairs=2)
            load_cells(j, pairs=2)

        ident = keep.tile([P, P], F32)
        make_identity(nc, ident[:])

        g_f32 = keep.tile([P, CH], F32)
        nc.scalar.mul(out=g_f32[:], in_=g_sb[:], mul=-1.0)
        g_ps = psum_t.tile([P, PACK, P], F32, tag="x_t")
        for t in range(PACK):
            nc.tensor.transpose(g_ps[:, t, :], g_f32[:, t * P : (t + 1) * P], ident[:])
        g_t = keep.tile([P, P, PACK], F32)
        nc.scalar.copy(out=g_t[:], in_=g_ps[:].rearrange("p t b -> p b t"))

        w_grouped = keep.tile([P, SIZE, PACK], BF16, align_bytes=64)
        w_codes = keep.tile([P, SIZE], U32, align_bytes=64)
        w_scales = keep.tile([P, SIZE], U8, align_bytes=64)

        def group_w(h):
            cols = slice(h * N_TILE, (h + 1) * N_TILE)
            nc.scalar.copy(out=w_grouped[:, cols, :], in_=w_raw[:, :, cols].rearrange("p t s -> p s t"))

        def quantise_w(h):
            cols = slice(h * N_TILE, (h + 1) * N_TILE)
            nc.vector.quantize_mx(
                out=w_codes[:, cols].bitcast(E4M3_X4),
                scales=w_scales[:, cols],
                in_=w_grouped[:, cols, :].rearrange("p s t -> p (s t)"),
            )

        da_codes = keep.tile([P, CHILDREN, P], U32, align_bytes=64)
        da_scales = keep.tile([P, CHILDREN, P], U8, align_bytes=64)
        slope = {}
        x_sb = {}
        x_t = {}
        da_bf = {}

        def gate_slope(j, pieces=1):
            slope[j] = work.tile([P, PAIR, CH], F32, name="slope", tag="slope")
            x_sb[j] = work.tile([P, PAIR, CH], F32, name="x_sb", tag="x_sb")
            step = PAIR // pieces
            for i in range(0, PAIR, step):
                nc.vector.scalar_tensor_tensor(
                    out=slope[j][:, i : i + step, :], in0=f_sb[j][:, i : i + step, :], scalar=1.0,
                    in1=f_sb[j][:, i : i + step, :], op0=ALU.subtract, op1=ALU.mult,
                )

        def gate_slope_child(j, i):
            if i == 0:
                slope[j] = work.tile([P, PAIR, CH], F32, name="slope", tag="slope")
                x_sb[j] = work.tile([P, PAIR, CH], F32, name="x_sb", tag="x_sb")
            nc.vector.scalar_tensor_tensor(
                out=slope[j][:, i, :], in0=f_sb[j][:, i, :], scalar=1.0, in1=f_sb[j][:, i, :],
                op0=ALU.subtract, op1=ALU.mult,
            )

        def times_cell(engine, j, cols):
            engine.tensor_tensor(
                out=x_sb[j][:].rearrange("p k c -> p (k c)")[:, cols],
                in0=slope[j][:].rearrange("p k c -> p (k c)")[:, cols],
                in1=ck_sb[j].rearrange("p k c -> p (k c)")[:, cols],
                op=ALU.mult,
            )

        def transpose_child(n):
            j, i = divmod(n, PAIR)
            x_t[n] = psum_t.tile([P, P, PACK], F32, name="x_t", tag="x_t")
            for t in range(PACK):
                nc.tensor.transpose(x_t[n][:, :, t], x_sb[j][:, i, t * P : (t + 1) * P], ident[:])

        def transpose_pair(j):
            for i in range(PAIR):
                transpose_child(j * PAIR + i)

        def times_grad(n):
            j, i = divmod(n, PAIR)
            if i == 0:
                da_bf[j] = work.tile([P, PAIR, P, PACK], BF16, name="da_bf", tag="da_bf", align_bytes=64)
            nc.vector.tensor_tensor(
                out=da_bf[j][:, i], in0=x_t[n][:], in1=g_t[:], op=ALU.mult
            )

        def quantise_pair(j):
            kids = slice(j * PAIR, (j + 1) * PAIR)
            nc.vector.quantize_mx(
                out=da_codes[:, kids, :].rearrange("p k b -> p (k b)").bitcast(E5M2_X4),
                scales=da_scales[:, kids, :].rearrange("p k b -> p (k b)"),
                in_=da_bf[j][:].rearrange("p k b t -> p (k b t)"),
            )

        def quantise_child(n):
            j, i = divmod(n, PAIR)
            nc.vector.quantize_mx(
                out=da_codes[:, n, :].bitcast(E5M2_X4),
                scales=da_scales[:, n, :],
                in_=da_bf[j][:, i].rearrange("p b t -> p (b t)"),
            )

        waiting = []

        out_pair = {}

        def multiply(n):
            j, i = divmod(n, PAIR)
            if i == 0:
                out_pair[j] = keep.tile([P, PAIR, SIZE], F32, name="out_pair%d" % j)
            out_sb = out_pair[j][:, i, :]
            for h in range(HALVES):
                cols = slice(h * N_TILE, (h + 1) * N_TILE)
                acc = psum_o.tile([P, N_TILE], F32, name="acc", tag="acc")
                nc.tensor.matmul_mx(
                    out=acc[:],
                    lhsT=da_codes[:, n, :].bitcast(E5M2_X4),
                    lhsT_scale=da_scales[:, n, :],
                    rhs=w_codes[:, cols].bitcast(E4M3_X4),
                    rhs_scale=w_scales[:, cols],
                    start=True,
                    stop=True,
                )
                if n >= VECTOR_FROM and h == HALVES - 1:
                    waiting.append((n, out_sb, acc))
                else:
                    nc.scalar.copy(out=out_sb[:, cols], in_=acc[:])
                    if n >= FINE_FROM:
                        nc.sync.dma_start(out=out[:, n, cols], in_=out_sb[:, cols])
            if n < COARSE_BELOW:
                if i == PAIR - 1:
                    nc.sync.dma_start(out=out[:, j * PAIR : (j + 1) * PAIR, :], in_=out_pair[j][:])
            elif n < FINE_FROM:
                nc.sync.dma_start(out=out[:, n, :], in_=out_sb)

        def passes(n):
            j, i = divmod(n, PAIR)
            if i == 0:
                out_pair[j] = keep.tile([P, PAIR, SIZE], F32, name="out_pair%d" % j)
            banks = []
            for h in range(HALVES):
                cols = slice(h * N_TILE, (h + 1) * N_TILE)
                acc = psum_o.tile([P, N_TILE], F32, name="acc", tag="acc")
                nc.tensor.matmul_mx(
                    out=acc[:],
                    lhsT=da_codes[:, n, :].bitcast(E5M2_X4),
                    lhsT_scale=da_scales[:, n, :],
                    rhs=w_codes[:, cols].bitcast(E4M3_X4),
                    rhs_scale=w_scales[:, cols],
                    start=True,
                    stop=True,
                )
                banks.append(acc)
            return banks

        def empty_and_store(on_vector, n, h, acc):
            j, i = divmod(n, PAIR)
            cols = slice(h * N_TILE, (h + 1) * N_TILE)
            if on_vector:
                nc.vector.tensor_copy(out=out_pair[j][:, i, cols], in_=acc[:])
            else:
                nc.scalar.copy(out=out_pair[j][:, i, cols], in_=acc[:])
            nc.sync.dma_start(out=out[:, n, cols], in_=out_pair[j][:, i, cols])

        def vector_empties():
            cols = slice(N_TILE, SIZE)
            for n, out_sb, acc in waiting:
                nc.vector.tensor_copy(out=out_sb[:, cols], in_=acc[:])
                nc.sync.dma_start(out=out[:, n, cols], in_=out_sb[:, cols])
            waiting.clear()

        gate_slope(0, pieces=PAIR)
        for i in range(PAIR):
            times_cell(nc.vector, 0, slice(i * CH, (i + 1) * CH))
            transpose_child(i)
        for h in range(HALVES):
            group_w(h)
        state = {"multiplied": 0}

        def finish_pair(j):
            quantise_pair(j)
            if j == W_PAIR:
                for h in range(HALVES):
                    quantise_w(h)
            if j >= W_PAIR:
                due = min((j + 1) * PAIR, state["multiplied"] + CATCH_UP)
                for m in range(state["multiplied"], due):
                    multiply(m)
                state["multiplied"] = due

        for j in range(PAIRS):
            kids = range(j * PAIR, (j + 1) * PAIR)
            more = j + 1 < PAIRS
            if more:
                gate_slope_child(j + 1, 0)
            if j > 0:
                finish_pair(j - 1)
            if more:
                gate_slope_child(j + 1, 1)
                times_cell(nc.gpsimd, j + 1, slice(CH, PAIR * CH))
                times_cell(nc.vector, j + 1, slice(0, CH))
                transpose_child((j + 1) * PAIR)
            for n in kids:
                times_grad(n)
            if more:
                transpose_child((j + 1) * PAIR + 1)
            if j == PAIRS - 2:
                break
        last = CHILDREN - 2 * PAIR
        assert state["multiplied"] == last
        banks = {}
        quantise_child(last)
        banks[last] = passes(last)
        empty_and_store(False, last, 0, banks[last][0])
        empty_and_store(False, last, 1, banks[last][1])
        times_grad(last + 2)
        quantise_child(last + 1)
        banks[last + 1] = passes(last + 1)
        empty_and_store(False, last + 1, 0, banks[last + 1][0])
        times_grad(last + 3)
        quantise_child(last + 2)
        banks[last + 2] = passes(last + 2)
        quantise_child(last + 3)
        banks[last + 3] = passes(last + 3)
        empty_and_store(True, last + 1, 1, banks[last + 1][1])
        for n in (last + 2, last + 3):
            empty_and_store(False, n, 0, banks[n][0])
            empty_and_store(True, n, 1, banks[n][1])
        multiplied = CHILDREN
        assert multiplied == CHILDREN
